import numpy as np
import ml_dtypes


def mxq(x, axis, fmt="e4m3"):
    dtype, down = {"e4m3": (ml_dtypes.float8_e4m3fn, 7), "e5m2": (ml_dtypes.float8_e5m2, 14)}[fmt]
    v = np.moveaxis(np.asarray(x, np.float32).astype(ml_dtypes.bfloat16).astype(np.float64), axis, -1)
    blocks = v.reshape(v.shape[:-1] + (-1, 32))
    amax = np.abs(blocks).max(-1, keepdims=True)
    byte = np.maximum(np.where(amax > 0, np.frexp(amax)[1] - 1 + 127, 0) - down, 1)
    scale = np.exp2(byte - 127.0)
    codes = (blocks / scale).astype(np.float32).astype(dtype).astype(np.float64)
    return np.moveaxis((codes * scale).reshape(v.shape), -1, axis)


WIDE = False


def mx_kscale(k):
    if not WIDE:
        return np.ones(k)
    levels = np.array([10, -10, 5, -5, 0])
    a = np.random.permutation(np.resize(levels, k // 512 * 4)).reshape(k // 512, 4)
    idx = np.arange(k)
    return np.exp2(a[idx // 512, idx % 128 // 32])


BF16 = ml_dtypes.bfloat16


def bf(x):
    return np.asarray(x, np.float32).astype(BF16)


def f64(x):
    return np.asarray(x).astype(np.float64)


BS, CIN, COUT, OUT_DIM, BLK = 128, 128, 128, 96, 4
D = OUT_DIM * BLK
K = CIN * BLK


def setup_inputs():
    s = mx_kscale(K)
    sd = np.tile(s.reshape(CIN, 1, BLK), (1, OUT_DIM, 1)).reshape(CIN, D)
    return {"x": bf(np.random.standard_normal((BS, CIN, D)) * sd),
            "weight": bf(np.random.standard_normal((COUT, CIN, D)) / sd)}


def reference(x, weight):
    bs, cin, d = x.shape
    cout = weight.shape[0]
    n = d // BLK
    xr = f64(x).reshape(bs, cin, n, BLK).transpose(2, 0, 1, 3).reshape(n, bs, cin * BLK)
    wr = f64(weight).reshape(cout, cin, n, BLK).transpose(2, 1, 3, 0).reshape(n, cin * BLK, cout)
    out = mxq(xr, 2, "e4m3") @ mxq(wr, 1, "e4m3")
    return out.transpose(1, 2, 0) / np.sqrt(cin)

@@ -1,0 +1,172 @@
+from contextlib import ExitStack
+import math
+
+import concourse.mybir as mybir
+
+F32 = mybir.dt.float32
+BF16 = mybir.dt.bfloat16
+U32 = mybir.dt.uint32
+U8 = mybir.dt.uint8
+FP8X4 = mybir.dt.float8_e4m3fn_x4
+
+P = 128
+NPOS = 96
+BLK = 4
+D = NPOS * BLK
+CH = 16
+NCH = 8
+G = 32
+R = P // G
+FLOPS = 2 * NPOS * 128 * 128 * 512
+MANUAL = True
+INV = 1.0 / math.sqrt(128.0)
+
+
+def tile_nonoverlappinglocallyconnected1d_kernel(tc, x, weight, out):
+    nc = tc.nc
+    with ExitStack() as ctx:
+        keep = ctx.enter_context(tc.tile_pool(name="keep", bufs=1))
+        rawp = ctx.enter_context(tc.tile_pool(name="rawp", bufs=3))
+        big = ctx.enter_context(tc.tile_pool(name="big", bufs=8))
+        wq = ctx.enter_context(tc.tile_pool(name="wq", bufs=4))
+        psum = ctx.enter_context(tc.psum_pool(name="psum", bufs=8))
+        if MANUAL:
+            ctx.enter_context(tc.manual_schedule())
+
+        xcodes = keep.tile([P, NPOS, P], U32, name="xcodes", align_bytes=64)
+        xsc = keep.tile([P, NPOS, P], U8, name="xsc", align_bytes=64)
+
+        raws = {}
+        xg = {}
+        wg = {}
+        wcs = {}
+        osbs = {}
+
+        def load(k):
+            src = x if k < NCH else weight
+            r0 = CH * (k % NCH)
+            t = rawp.tile([P, CH * D], BF16, tag="raw", name="raw%d" % k)
+            nc.sync.dma_start(
+                out=t[:].rearrange("p (b d) -> p b d", b=CH),
+                in_=src[r0:r0 + CH].rearrange("b i d -> i b d"),
+            )
+            raws[k] = t
+
+        def words(k):
+            return raws[k][:].bitcast(F32).rearrange("p (b n u) -> p n b u", b=CH, n=NPOS, u=2)
+
+        def regroup_x(k):
+            h, cc = divmod(k, 4)
+            if cc == 0:
+                xg[h] = [
+                    big.tile([P, 6144], BF16, tag="big", name="xg%d_%d" % (h, q), align_bytes=64)
+                    for q in range(4)
+                ]
+            src = words(k)
+            for q in range(4):
+                dst = xg[h][q][:].bitcast(F32).rearrange("p (n b u) -> p n b u", n=24, b=64, u=2)
+                o_ap = dst[:, :, CH * cc:CH * cc + CH, :]
+                i_ap = src[:, 24 * q:24 * q + 24, :, :]
+                if q == 0:
+                    nc.vector.tensor_copy(out=o_ap, in_=i_ap)
+                else:
+                    nc.scalar.copy(out=o_ap, in_=i_ap)
+
+        def quant_x(h, q):
+            for nl in range(24):
+                n = 24 * q + nl
+                nc.vector.quantize_mx(
+                    out=xcodes[:, n, 64 * h:64 * h + 64].bitcast(FP8X4),
+                    scales=xsc[:, n, 64 * h:64 * h + 64],
+                    in_=xg[h][q][:, 256 * nl:256 * nl + 256],
+                )
+
+        def regroup_w(k, scalar_tiles):
+            gi, oc = divmod(k - NCH, 2)
+            if oc == 0:
+                wg[gi] = [
+                    big.tile([P, 6144], BF16, tag="big", name="wg%d_%d" % (gi, t), align_bytes=64)
+                    for t in range(2)
+                ]
+            src = words(k)
+            for t in range(2):
+                dst = wg[gi][t][:].bitcast(F32).rearrange("p (w r o u) -> p r w o u", w=12, r=R, o=G, u=2)
+                if t in scalar_tiles:
+                    for r in range(R):
+                        n0 = 48 * t + 12 * r
+                        nc.scalar.copy(
+                            out=dst[:, r, :, CH * oc:CH * oc + CH, :],
+                            in_=src[:, n0:n0 + 12, :, :],
+                        )
+                else:
+                    nc.vector.tensor_copy(
+                        out=dst[:, :, :, CH * oc:CH * oc + CH, :],
+                        in_=src[:, 48 * t:48 * t + 48, :, :].rearrange("p (r w) o u -> p r w o u", r=R),
+                    )
+
+        def quant_w(gi, t):
+            wc = wq.tile([P, 1536], U32, tag="wc", name="wc%d_%d" % (gi, t), align_bytes=64)
+            ws = wq.tile([P, 1536], U8, tag="ws", name="ws%d_%d" % (gi, t), align_bytes=64)
+            for a in range(3):
+                nc.vector.quantize_mx(
+                    out=wc[:, 512 * a:512 * a + 512].bitcast(FP8X4),
+                    scales=ws[:, 512 * a:512 * a + 512],
+                    in_=wg[gi][t][:, 2048 * a:2048 * a + 2048],
+                )
+            wcs[(gi, t)] = (wc, ws)
+
+        def passes(gi, t):
+            if t == 0:
+                osbs[gi] = big.tile([P, G, NPOS], F32, tag="big", name="osb%d" % gi, align_bytes=64)
+            osb = osbs[gi]
+            wc, ws = wcs[(gi, t)]
+            for a in range(3):
+                for r in range(R):
+                    n0 = 48 * t + 12 * r + 4 * a
+                    ps = psum.tile([P, 4, P], F32, tag="ps", name="ps%d_%d_%d_%d" % (gi, t, a, r))
+                    for j in range(4):
+                        wl = 4 * a + j
+                        nc.tensor.matmul_mx(
+                            out=ps[:, j, :],
+                            lhsT=xcodes[:, n0 + j, :].bitcast(FP8X4),
+                            lhsT_scale=xsc[:, n0 + j, :],
+                            rhs=wc[:, P * wl:P * wl + P].bitcast(FP8X4),
+                            rhs_scale=ws[:, P * wl:P * wl + P],
+                            start=True,
+                            stop=True,
+                        )
+                    nc.scalar.mul(
+                        out=osb[:, :, n0:n0 + 4],
+                        in_=ps[:, :, G * r:G * r + G].rearrange("p j c -> p c j"),
+                        mul=INV,
+                    )
+
+        for k in range(3):
+            load(k)
+        for k in range(2 * NCH):
+            if k < NCH:
+                regroup_x(k)
+            else:
+                regroup_w(k, (1,) if k < NCH + 2 else ())
+            if k + 3 < 2 * NCH:
+                load(k + 3)
+            if k == 3:
+                quant_x(0, 0)
+                quant_x(0, 1)
+            elif k == 4:
+                quant_x(0, 2)
+            elif k == 5:
+                quant_x(0, 3)
+            elif k == 7:
+                quant_x(1, 0)
+                quant_x(1, 1)
+            elif k == 8:
+                quant_x(1, 2)
+                quant_x(1, 3)
+            elif k > 8 and k % 2 == 1:
+                gi = (k - NCH) // 2
+                for t in range(2):
+                    quant_w(gi, t)
+                    passes(gi, t)
+        for gi in range(4):
+            nc.sync.dma_start(out=out[:, G * gi:G * gi + G, :], in_=osbs[gi][:])

@@ -17,8 +17,9 @@ CH = 16
 NCH = 8
 G = 32
 R = P // G
+RAWB = 4
+RV_V = 3
 FLOPS = 2 * NPOS * 128 * 128 * 512
-MANUAL = True
 INV = 1.0 / math.sqrt(128.0)
 
 
@@ -26,12 +27,11 @@ def tile_nonoverlappinglocallyconnected1d_kernel(tc, x, weight, out):
     nc = tc.nc
     with ExitStack() as ctx:
         keep = ctx.enter_context(tc.tile_pool(name="keep", bufs=1))
-        rawp = ctx.enter_context(tc.tile_pool(name="rawp", bufs=3))
+        rawp = ctx.enter_context(tc.tile_pool(name="rawp", bufs=RAWB))
         big = ctx.enter_context(tc.tile_pool(name="big", bufs=8))
         wq = ctx.enter_context(tc.tile_pool(name="wq", bufs=4))
         psum = ctx.enter_context(tc.psum_pool(name="psum", bufs=8))
-        if MANUAL:
-            ctx.enter_context(tc.manual_schedule())
+        ctx.enter_context(tc.manual_schedule())
 
         xcodes = keep.tile([P, NPOS, P], U32, name="xcodes", align_bytes=64)
         xsc = keep.tile([P, NPOS, P], U8, name="xsc", align_bytes=64)
@@ -67,7 +67,7 @@ def tile_nonoverlappinglocallyconnected1d_kernel(tc, x, weight, out):
                 dst = xg[h][q][:].bitcast(F32).rearrange("p (n b u) -> p n b u", n=24, b=64, u=2)
                 o_ap = dst[:, :, CH * cc:CH * cc + CH, :]
                 i_ap = src[:, 24 * q:24 * q + 24, :, :]
-                if q == 0:
+                if q < 2:
                     nc.vector.tensor_copy(out=o_ap, in_=i_ap)
                 else:
                     nc.scalar.copy(out=o_ap, in_=i_ap)
@@ -81,7 +81,7 @@ def tile_nonoverlappinglocallyconnected1d_kernel(tc, x, weight, out):
                     in_=xg[h][q][:, 256 * nl:256 * nl + 256],
                 )
 
-        def regroup_w(k, scalar_tiles):
+        def regroup_w(k):
             gi, oc = divmod(k - NCH, 2)
             if oc == 0:
                 wg[gi] = [
@@ -91,17 +91,15 @@ def tile_nonoverlappinglocallyconnected1d_kernel(tc, x, weight, out):
             src = words(k)
             for t in range(2):
                 dst = wg[gi][t][:].bitcast(F32).rearrange("p (w r o u) -> p r w o u", w=12, r=R, o=G, u=2)
-                if t in scalar_tiles:
-                    for r in range(R):
-                        n0 = 48 * t + 12 * r
-                        nc.scalar.copy(
-                            out=dst[:, r, :, CH * oc:CH * oc + CH, :],
-                            in_=src[:, n0:n0 + 12, :, :],
-                        )
-                else:
-                    nc.vector.tensor_copy(
-                        out=dst[:, :, :, CH * oc:CH * oc + CH, :],
-                        in_=src[:, 48 * t:48 * t + 48, :, :].rearrange("p (r w) o u -> p r w o u", r=R),
+                nc.vector.tensor_copy(
+                    out=dst[:, 0:RV_V, :, CH * oc:CH * oc + CH, :],
+                    in_=src[:, 48 * t:48 * t + 12 * RV_V, :, :].rearrange("p (r w) o u -> p r w o u", r=RV_V),
+                )
+                for r in range(RV_V, R):
+                    n0 = 48 * t + 12 * r
+                    nc.scalar.copy(
+                        out=dst[:, r, :, CH * oc:CH * oc + CH, :],
+                        in_=src[:, n0:n0 + 12, :, :],
                     )
 
         def quant_w(gi, t):
@@ -115,41 +113,44 @@ def tile_nonoverlappinglocallyconnected1d_kernel(tc, x, weight, out):
                 )
             wcs[(gi, t)] = (wc, ws)
 
-        def passes(gi, t):
-            if t == 0:
+        def bank(gi, idx):
+            t, rest = divmod(idx, 12)
+            a, r = divmod(rest, R)
+            if idx == 0:
                 osbs[gi] = big.tile([P, G, NPOS], F32, tag="big", name="osb%d" % gi, align_bytes=64)
             osb = osbs[gi]
             wc, ws = wcs[(gi, t)]
-            for a in range(3):
-                for r in range(R):
-                    n0 = 48 * t + 12 * r + 4 * a
-                    ps = psum.tile([P, 4, P], F32, tag="ps", name="ps%d_%d_%d_%d" % (gi, t, a, r))
-                    for j in range(4):
-                        wl = 4 * a + j
-                        nc.tensor.matmul_mx(
-                            out=ps[:, j, :],
-                            lhsT=xcodes[:, n0 + j, :].bitcast(FP8X4),
-                            lhsT_scale=xsc[:, n0 + j, :],
-                            rhs=wc[:, P * wl:P * wl + P].bitcast(FP8X4),
-                            rhs_scale=ws[:, P * wl:P * wl + P],
-                            start=True,
-                            stop=True,
-                        )
-                    nc.scalar.mul(
-                        out=osb[:, :, n0:n0 + 4],
-                        in_=ps[:, :, G * r:G * r + G].rearrange("p j c -> p c j"),
-                        mul=INV,
-                    )
+            n0 = 48 * t + 12 * r + 4 * a
+            ps = psum.tile([P, 4, P], F32, tag="ps", name="ps%d_%d" % (gi, idx))
+            for j in range(4):
+                wl = 4 * a + j
+                nc.tensor.matmul_mx(
+                    out=ps[:, j, :],
+                    lhsT=xcodes[:, n0 + j, :].bitcast(FP8X4),
+                    lhsT_scale=xsc[:, n0 + j, :],
+                    rhs=wc[:, P * wl:P * wl + P].bitcast(FP8X4),
+                    rhs_scale=ws[:, P * wl:P * wl + P],
+                    start=True,
+                    stop=True,
+                )
+            nc.scalar.mul(
+                out=osb[:, :, n0:n0 + 4],
+                in_=ps[:, :, G * r:G * r + G].rearrange("p j c -> p c j"),
+                mul=INV,
+            )
 
-        for k in range(3):
-            load(k)
-        for k in range(2 * NCH):
+        def step(k):
             if k < NCH:
                 regroup_x(k)
             else:
-                regroup_w(k, (1,) if k < NCH + 2 else ())
-            if k + 3 < 2 * NCH:
-                load(k + 3)
+                regroup_w(k)
+            if k + RAWB < 2 * NCH:
+                load(k + RAWB)
+
+        for k in range(RAWB):
+            load(k)
+        for k in range(10):
+            step(k)
             if k == 3:
                 quant_x(0, 0)
                 quant_x(0, 1)
@@ -163,10 +164,16 @@ def tile_nonoverlappinglocallyconnected1d_kernel(tc, x, weight, out):
             elif k == 8:
                 quant_x(1, 2)
                 quant_x(1, 3)
-            elif k > 8 and k % 2 == 1:
-                gi = (k - NCH) // 2
-                for t in range(2):
-                    quant_w(gi, t)
-                    passes(gi, t)
+        for gi in range(4):
+            quant_w(gi, 0)
+            quant_w(gi, 1)
+            for idx in range(8):
+                bank(gi, idx)
+            if gi < 3:
+                step(10 + 2 * gi)
+            for idx in range(8, 24):
+                bank(gi, idx)
+            if gi < 3:
+                step(11 + 2 * gi)
         for gi in range(4):
             nc.sync.dma_start(out=out[:, G * gi:G * gi + G, :], in_=osbs[gi][:])

@@ -15,10 +15,9 @@ BLK = 4
 D = NPOS * BLK
 CH = 16
 NCH = 8
-G = 32
-R = P // G
 RAWB = 4
-RV_V = 3
+W = 24
+GROUPS = (64, 32, 32)
 FLOPS = 2 * NPOS * 128 * 128 * 512
 INV = 1.0 / math.sqrt(128.0)
 
@@ -28,8 +27,8 @@ def tile_nonoverlappinglocallyconnected1d_kernel(tc, x, weight, out):
     with ExitStack() as ctx:
         keep = ctx.enter_context(tc.tile_pool(name="keep", bufs=1))
         rawp = ctx.enter_context(tc.tile_pool(name="rawp", bufs=RAWB))
-        big = ctx.enter_context(tc.tile_pool(name="big", bufs=8))
-        wq = ctx.enter_context(tc.tile_pool(name="wq", bufs=4))
+        big = ctx.enter_context(tc.tile_pool(name="big", bufs=4))
+        wq = ctx.enter_context(tc.tile_pool(name="wq", bufs=2))
         psum = ctx.enter_context(tc.psum_pool(name="psum", bufs=8))
         ctx.enter_context(tc.manual_schedule())
 
@@ -59,15 +58,16 @@ def tile_nonoverlappinglocallyconnected1d_kernel(tc, x, weight, out):
             h, cc = divmod(k, 4)
             if cc == 0:
                 xg[h] = [
-                    big.tile([P, 6144], BF16, tag="big", name="xg%d_%d" % (h, q), align_bytes=64)
-                    for q in range(4)
+                    big.tile([P, 12288], BF16, tag="big", name="xg%d_%d" % (h, e), align_bytes=64)
+                    for e in range(2)
                 ]
             src = words(k)
             for q in range(4):
-                dst = xg[h][q][:].bitcast(F32).rearrange("p (n b u) -> p n b u", n=24, b=64, u=2)
-                o_ap = dst[:, :, CH * cc:CH * cc + CH, :]
+                dst = xg[h][q // 2][:].bitcast(F32).rearrange("p (n b u) -> p n b u", n=48, b=64, u=2)
+                nl = 24 * (q % 2)
+                o_ap = dst[:, nl:nl + 24, CH * cc:CH * cc + CH, :]
                 i_ap = src[:, 24 * q:24 * q + 24, :, :]
-                if q < 2:
+                if q == 0:
                     nc.vector.tensor_copy(out=o_ap, in_=i_ap)
                 else:
                     nc.scalar.copy(out=o_ap, in_=i_ap)
@@ -75,82 +75,95 @@ def tile_nonoverlappinglocallyconnected1d_kernel(tc, x, weight, out):
         def quant_x(h, q):
             for nl in range(24):
                 n = 24 * q + nl
+                c0 = 256 * (n % 48)
                 nc.vector.quantize_mx(
                     out=xcodes[:, n, 64 * h:64 * h + 64].bitcast(FP8X4),
                     scales=xsc[:, n, 64 * h:64 * h + 64],
-                    in_=xg[h][q][:, 256 * nl:256 * nl + 256],
+                    in_=xg[h][q // 2][:, c0:c0 + 256],
                 )
 
-        def regroup_w(k):
-            gi, oc = divmod(k - NCH, 2)
-            if oc == 0:
-                wg[gi] = [
-                    big.tile([P, 6144], BF16, tag="big", name="wg%d_%d" % (gi, t), align_bytes=64)
-                    for t in range(2)
-                ]
-            src = words(k)
-            for t in range(2):
-                dst = wg[gi][t][:].bitcast(F32).rearrange("p (w r o u) -> p r w o u", w=12, r=R, o=G, u=2)
-                nc.vector.tensor_copy(
-                    out=dst[:, 0:RV_V, :, CH * oc:CH * oc + CH, :],
-                    in_=src[:, 48 * t:48 * t + 12 * RV_V, :, :].rearrange("p (r w) o u -> p r w o u", r=RV_V),
-                )
-                for r in range(RV_V, R):
-                    n0 = 48 * t + 12 * r
+        chunk_of = {}
+        first_o = []
+        kk = NCH
+        oo = 0
+        for gi in range(len(GROUPS)):
+            first_o.append(oo)
+            for oc in range(GROUPS[gi] // CH):
+                chunk_of[kk] = (gi, oc)
+                kk += 1
+            oo += GROUPS[gi]
+
+        def regroup_w(k, v, w0, w1, on_scalar):
+            gi, oc = chunk_of[k]
+            g = GROUPS[gi]
+            r_n = P // g
+            if (gi, v) not in wg:
+                wg[(gi, v)] = big.tile([P, 12288], BF16, tag="big", name="wg%d_%d" % (gi, v), align_bytes=64)
+            dst = wg[(gi, v)][:].bitcast(F32).rearrange("p (w r o u) -> p r w o u", w=W, r=r_n, o=g, u=2)
+            base = W * r_n * v
+            src = words(k)[:, base:base + W * r_n, :, :].rearrange("p (r w) o u -> p r w o u", r=r_n)
+            if on_scalar:
+                for r in range(r_n):
                     nc.scalar.copy(
-                        out=dst[:, r, :, CH * oc:CH * oc + CH, :],
-                        in_=src[:, n0:n0 + 12, :, :],
+                        out=dst[:, r, w0:w1, CH * oc:CH * oc + CH, :],
+                        in_=src[:, r, w0:w1, :, :],
                     )
-
-        def quant_w(gi, t):
-            wc = wq.tile([P, 1536], U32, tag="wc", name="wc%d_%d" % (gi, t), align_bytes=64)
-            ws = wq.tile([P, 1536], U8, tag="ws", name="ws%d_%d" % (gi, t), align_bytes=64)
-            for a in range(3):
-                nc.vector.quantize_mx(
-                    out=wc[:, 512 * a:512 * a + 512].bitcast(FP8X4),
-                    scales=ws[:, 512 * a:512 * a + 512],
-                    in_=wg[gi][t][:, 2048 * a:2048 * a + 2048],
+            else:
+                nc.vector.tensor_copy(
+                    out=dst[:, :, w0:w1, CH * oc:CH * oc + CH, :],
+                    in_=src[:, :, w0:w1, :, :],
                 )
-            wcs[(gi, t)] = (wc, ws)
 
-        def bank(gi, idx):
-            t, rest = divmod(idx, 12)
-            a, r = divmod(rest, R)
-            if idx == 0:
-                osbs[gi] = big.tile([P, G, NPOS], F32, tag="big", name="osb%d" % gi, align_bytes=64)
-            osb = osbs[gi]
-            wc, ws = wcs[(gi, t)]
-            n0 = 48 * t + 12 * r + 4 * a
-            ps = psum.tile([P, 4, P], F32, tag="ps", name="ps%d_%d" % (gi, idx))
-            for j in range(4):
-                wl = 4 * a + j
-                nc.tensor.matmul_mx(
-                    out=ps[:, j, :],
-                    lhsT=xcodes[:, n0 + j, :].bitcast(FP8X4),
-                    lhsT_scale=xsc[:, n0 + j, :],
-                    rhs=wc[:, P * wl:P * wl + P].bitcast(FP8X4),
-                    rhs_scale=ws[:, P * wl:P * wl + P],
-                    start=True,
-                    stop=True,
-                )
-            nc.scalar.mul(
-                out=osb[:, :, n0:n0 + 4],
-                in_=ps[:, :, G * r:G * r + G].rearrange("p j c -> p c j"),
-                mul=INV,
+        def quant_w(gi, v, a):
+            if a == 0:
+                wc = wq.tile([P, W * P], U32, tag="wc", name="wc%d_%d" % (gi, v), align_bytes=64)
+                ws = wq.tile([P, W * P], U8, tag="ws", name="ws%d_%d" % (gi, v), align_bytes=64)
+                wcs[(gi, v)] = (wc, ws)
+            wc, ws = wcs[(gi, v)]
+            nc.vector.quantize_mx(
+                out=wc[:, 512 * a:512 * a + 512].bitcast(FP8X4),
+                scales=ws[:, 512 * a:512 * a + 512],
+                in_=wg[(gi, v)][:, 2048 * a:2048 * a + 2048],
             )
 
-        def step(k):
-            if k < NCH:
-                regroup_x(k)
-            else:
-                regroup_w(k)
+        def banks(gi, v, a):
+            g = GROUPS[gi]
+            r_n = P // g
+            half = first_o[gi] // 64
+            if half not in osbs:
+                osbs[half] = big.tile([P, 64, NPOS], F32, tag="big", name="osb%d" % half, align_bytes=64)
+            osb = osbs[half]
+            ol = first_o[gi] % 64
+            wc, ws = wcs[(gi, v)]
+            for r in range(r_n):
+                n0 = W * r_n * v + W * r + 4 * a
+                ps = psum.tile([P, 4, P], F32, tag="ps", name="ps%d_%d_%d_%d" % (gi, v, a, r))
+                for j in range(4):
+                    wl = 4 * a + j
+                    nc.tensor.matmul_mx(
+                        out=ps[:, j, :],
+                        lhsT=xcodes[:, n0 + j, :].bitcast(FP8X4),
+                        lhsT_scale=xsc[:, n0 + j, :],
+                        rhs=wc[:, P * wl:P * wl + P].bitcast(FP8X4),
+                        rhs_scale=ws[:, P * wl:P * wl + P],
+                        start=True,
+                        stop=True,
+                    )
+                nc.scalar.mul(
+                    out=osb[:, ol:ol + g, n0:n0 + 4],
+                    in_=ps[:, :, g * r:g * r + g].rearrange("p j c -> p c j"),
+                    mul=INV,
+                )
+
+        def next_load(k):
             if k + RAWB < 2 * NCH:
                 load(k + RAWB)
 
         for k in range(RAWB):
             load(k)
-        for k in range(10):
-            step(k)
+        for k in range(NCH):
+            regroup_x(k)
+            next_load(k)
             if k == 3:
                 quant_x(0, 0)
                 quant_x(0, 1)
@@ -161,19 +174,36 @@ def tile_nonoverlappinglocallyconnected1d_kernel(tc, x, weight, out):
             elif k == 7:
                 quant_x(1, 0)
                 quant_x(1, 1)
-            elif k == 8:
+        for k in range(8, 12):
+            regroup_w(k, 0, 0, W, False)
+            regroup_w(k, 1, 0, W, True)
+            next_load(k)
+            if k == 8:
                 quant_x(1, 2)
                 quant_x(1, 3)
-        for gi in range(4):
-            quant_w(gi, 0)
-            quant_w(gi, 1)
-            for idx in range(8):
-                bank(gi, idx)
-            if gi < 3:
-                step(10 + 2 * gi)
-            for idx in range(8, 24):
-                bank(gi, idx)
-            if gi < 3:
-                step(11 + 2 * gi)
-        for gi in range(4):
-            nc.sync.dma_start(out=out[:, G * gi:G * gi + G, :], in_=osbs[gi][:])
+        for v in range(2):
+            for a in range(6):
+                quant_w(0, v, a)
+                banks(0, v, a)
+            k = 12 + v
+            if v == 0:
+                regroup_w(k, 0, 0, W, False)
+                next_load(k)
+        for gi in (1, 2):
+            k = 11 + 2 * gi
+            regroup_w(k, 0, 0, W // 2, False)
+            for a in range(3):
+                quant_w(gi, 0, a)
+                banks(gi, 0, a)
+            regroup_w(k, 0, W // 2, W, False)
+            next_load(k)
+            for a in range(3, 6):
+                quant_w(gi, 0, a)
+                banks(gi, 0, a)
+            if gi == 1:
+                regroup_w(14, 0, 0, W, False)
+                next_load(14)
+        nc.sync.dma_start(out=out[:, 0:32, :], in_=osbs[0][:, 0:32, :])
+        nc.sync.dma_start(out=out[:, 32:64, :], in_=osbs[0][:, 32:64, :])
+        nc.sync.dma_start(out=out[:, 64:96, :], in_=osbs[1][:, 0:32, :])
+        nc.sync.dma_start(out=out[:, 96:128, :], in_=osbs[1][:, 32:64, :])

@@ -15,10 +15,10 @@ BLK = 4
 D = NPOS * BLK
 CH = 16
 NCH = 8
-RAWB = 4
-W = 24
-GROUPS = (64, 32, 32)
+G = 32
+R = P // G
 FLOPS = 2 * NPOS * 128 * 128 * 512
+RAWB = 4
 INV = 1.0 / math.sqrt(128.0)
 
 
@@ -27,8 +27,8 @@ def tile_nonoverlappinglocallyconnected1d_kernel(tc, x, weight, out):
     with ExitStack() as ctx:
         keep = ctx.enter_context(tc.tile_pool(name="keep", bufs=1))
         rawp = ctx.enter_context(tc.tile_pool(name="rawp", bufs=RAWB))
-        big = ctx.enter_context(tc.tile_pool(name="big", bufs=4))
-        wq = ctx.enter_context(tc.tile_pool(name="wq", bufs=2))
+        big = ctx.enter_context(tc.tile_pool(name="big", bufs=8))
+        wq = ctx.enter_context(tc.tile_pool(name="wq", bufs=4))
         psum = ctx.enter_context(tc.psum_pool(name="psum", bufs=8))
         ctx.enter_context(tc.manual_schedule())
 
@@ -58,14 +58,13 @@ def tile_nonoverlappinglocallyconnected1d_kernel(tc, x, weight, out):
             h, cc = divmod(k, 4)
             if cc == 0:
                 xg[h] = [
-                    big.tile([P, 12288], BF16, tag="big", name="xg%d_%d" % (h, e), align_bytes=64)
-                    for e in range(2)
+                    big.tile([P, 6144], BF16, tag="big", name="xg%d_%d" % (h, q), align_bytes=64)
+                    for q in range(4)
                 ]
             src = words(k)
             for q in range(4):
-                dst = xg[h][q // 2][:].bitcast(F32).rearrange("p (n b u) -> p n b u", n=48, b=64, u=2)
-                nl = 24 * (q % 2)
-                o_ap = dst[:, nl:nl + 24, CH * cc:CH * cc + CH, :]
+                dst = xg[h][q][:].bitcast(F32).rearrange("p (n b u) -> p n b u", n=24, b=64, u=2)
+                o_ap = dst[:, :, CH * cc:CH * cc + CH, :]
                 i_ap = src[:, 24 * q:24 * q + 24, :, :]
                 if q == 0:
                     nc.vector.tensor_copy(out=o_ap, in_=i_ap)
@@ -75,69 +74,50 @@ def tile_nonoverlappinglocallyconnected1d_kernel(tc, x, weight, out):
         def quant_x(h, q):
             for nl in range(24):
                 n = 24 * q + nl
-                c0 = 256 * (n % 48)
                 nc.vector.quantize_mx(
                     out=xcodes[:, n, 64 * h:64 * h + 64].bitcast(FP8X4),
                     scales=xsc[:, n, 64 * h:64 * h + 64],
-                    in_=xg[h][q // 2][:, c0:c0 + 256],
+                    in_=xg[h][q][:, 256 * nl:256 * nl + 256],
                 )
 
-        chunk_of = {}
-        first_o = []
-        kk = NCH
-        oo = 0
-        for gi in range(len(GROUPS)):
-            first_o.append(oo)
-            for oc in range(GROUPS[gi] // CH):
-                chunk_of[kk] = (gi, oc)
-                kk += 1
-            oo += GROUPS[gi]
-
-        def regroup_w(k, v, w0, w1, on_scalar):
-            gi, oc = chunk_of[k]
-            g = GROUPS[gi]
-            r_n = P // g
-            if (gi, v) not in wg:
-                wg[(gi, v)] = big.tile([P, 12288], BF16, tag="big", name="wg%d_%d" % (gi, v), align_bytes=64)
-            dst = wg[(gi, v)][:].bitcast(F32).rearrange("p (w r o u) -> p r w o u", w=W, r=r_n, o=g, u=2)
-            base = W * r_n * v
-            src = words(k)[:, base:base + W * r_n, :, :].rearrange("p (r w) o u -> p r w o u", r=r_n)
+        def regroup_w(k, t, a0, a1, on_scalar):
+            gi, oc = divmod(k - NCH, 2)
+            if (gi, t) not in wg:
+                wg[(gi, t)] = big.tile([P, 6144], BF16, tag="big", name="wg%d_%d" % (gi, t), align_bytes=64)
+            dst = wg[(gi, t)][:].bitcast(F32).rearrange("p (w r o u) -> p r w o u", w=12, r=R, o=G, u=2)
+            src = words(k)[:, 48 * t:48 * t + 48, :, :].rearrange("p (r w) o u -> p r w o u", r=R)
             if on_scalar:
-                for r in range(r_n):
+                for r in range(R):
                     nc.scalar.copy(
-                        out=dst[:, r, w0:w1, CH * oc:CH * oc + CH, :],
-                        in_=src[:, r, w0:w1, :, :],
+                        out=dst[:, r, 4 * a0:4 * a1, CH * oc:CH * oc + CH, :],
+                        in_=src[:, r, 4 * a0:4 * a1, :, :],
                     )
             else:
                 nc.vector.tensor_copy(
-                    out=dst[:, :, w0:w1, CH * oc:CH * oc + CH, :],
-                    in_=src[:, :, w0:w1, :, :],
+                    out=dst[:, :, 4 * a0:4 * a1, CH * oc:CH * oc + CH, :],
+                    in_=src[:, :, 4 * a0:4 * a1, :, :],
                 )
 
-        def quant_w(gi, v, a):
+        def quant_w(gi, t, a):
             if a == 0:
-                wc = wq.tile([P, W * P], U32, tag="wc", name="wc%d_%d" % (gi, v), align_bytes=64)
-                ws = wq.tile([P, W * P], U8, tag="ws", name="ws%d_%d" % (gi, v), align_bytes=64)
-                wcs[(gi, v)] = (wc, ws)
-            wc, ws = wcs[(gi, v)]
+                wc = wq.tile([P, 1536], U32, tag="wc", name="wc%d_%d" % (gi, t), align_bytes=64)
+                ws = wq.tile([P, 1536], U8, tag="ws", name="ws%d_%d" % (gi, t), align_bytes=64)
+                wcs[(gi, t)] = (wc, ws)
+            wc, ws = wcs[(gi, t)]
             nc.vector.quantize_mx(
                 out=wc[:, 512 * a:512 * a + 512].bitcast(FP8X4),
                 scales=ws[:, 512 * a:512 * a + 512],
-                in_=wg[(gi, v)][:, 2048 * a:2048 * a + 2048],
+                in_=wg[(gi, t)][:, 2048 * a:2048 * a + 2048],
             )
 
-        def banks(gi, v, a):
-            g = GROUPS[gi]
-            r_n = P // g
-            half = first_o[gi] // 64
-            if half not in osbs:
-                osbs[half] = big.tile([P, 64, NPOS], F32, tag="big", name="osb%d" % half, align_bytes=64)
-            osb = osbs[half]
-            ol = first_o[gi] % 64
-            wc, ws = wcs[(gi, v)]
-            for r in range(r_n):
-                n0 = W * r_n * v + W * r + 4 * a
-                ps = psum.tile([P, 4, P], F32, tag="ps", name="ps%d_%d_%d_%d" % (gi, v, a, r))
+        def passes(gi, t, a):
+            if gi not in osbs:
+                osbs[gi] = big.tile([P, G, NPOS], F32, tag="big", name="osb%d" % gi, align_bytes=64)
+            osb = osbs[gi]
+            wc, ws = wcs[(gi, t)]
+            for r in range(R):
+                n0 = 48 * t + 12 * r + 4 * a
+                ps = psum.tile([P, 4, P], F32, tag="ps", name="ps%d_%d_%d_%d" % (gi, t, a, r))
                 for j in range(4):
                     wl = 4 * a + j
                     nc.tensor.matmul_mx(
@@ -150,8 +130,8 @@ def tile_nonoverlappinglocallyconnected1d_kernel(tc, x, weight, out):
                         stop=True,
                     )
                 nc.scalar.mul(
-                    out=osb[:, ol:ol + g, n0:n0 + 4],
-                    in_=ps[:, :, g * r:g * r + g].rearrange("p j c -> p c j"),
+                    out=osb[:, :, n0:n0 + 4],
+                    in_=ps[:, :, G * r:G * r + G].rearrange("p j c -> p c j"),
                     mul=INV,
                 )
 
@@ -172,38 +152,23 @@ def tile_nonoverlappinglocallyconnected1d_kernel(tc, x, weight, out):
             elif k == 5:
                 quant_x(0, 3)
             elif k == 7:
-                quant_x(1, 0)
-                quant_x(1, 1)
-        for k in range(8, 12):
-            regroup_w(k, 0, 0, W, False)
-            regroup_w(k, 1, 0, W, True)
+                for q in range(4):
+                    quant_x(1, q)
+        regroup_w(NCH, 0, 0, 3, True)
+        regroup_w(NCH, 1, 0, 3, True)
+        next_load(NCH)
+        for gi in range(4):
+            k = NCH + 2 * gi + 1
+            regroup_w(k, 0, 0, 1, False)
+            for s in range(6):
+                if s < 5:
+                    regroup_w(k, (s + 1) // 3, (s + 1) % 3, (s + 1) % 3 + 1, False)
+                quant_w(gi, s // 3, s % 3)
+                passes(gi, s // 3, s % 3)
             next_load(k)
-            if k == 8:
-                quant_x(1, 2)
-                quant_x(1, 3)
-        for v in range(2):
-            for a in range(6):
-                quant_w(0, v, a)
-                banks(0, v, a)
-            k = 12 + v
-            if v == 0:
-                regroup_w(k, 0, 0, W, False)
-                next_load(k)
-        for gi in (1, 2):
-            k = 11 + 2 * gi
-            regroup_w(k, 0, 0, W // 2, False)
-            for a in range(3):
-                quant_w(gi, 0, a)
-                banks(gi, 0, a)
-            regroup_w(k, 0, W // 2, W, False)
-            next_load(k)
-            for a in range(3, 6):
-                quant_w(gi, 0, a)
-                banks(gi, 0, a)
-            if gi == 1:
-                regroup_w(14, 0, 0, W, False)
-                next_load(14)
-        nc.sync.dma_start(out=out[:, 0:32, :], in_=osbs[0][:, 0:32, :])
-        nc.sync.dma_start(out=out[:, 32:64, :], in_=osbs[0][:, 32:64, :])
-        nc.sync.dma_start(out=out[:, 64:96, :], in_=osbs[1][:, 0:32, :])
-        nc.sync.dma_start(out=out[:, 96:128, :], in_=osbs[1][:, 32:64, :])
+            if gi < 3:
+                regroup_w(k + 1, 0, 0, 3, False)
+                regroup_w(k + 1, 1, 0, 3, False)
+                next_load(k + 1)
+        for gi in range(4):
+            nc.sync.dma_start(out=out[:, G * gi:G * gi + G, :], in_=osbs[gi][:])

@@ -2,6 +2,7 @@ from contextlib import ExitStack
 import math
 
 import concourse.mybir as mybir
+from concourse.masks import make_identity
 
 F32 = mybir.dt.float32
 BF16 = mybir.dt.bfloat16
@@ -13,79 +14,103 @@ P = 128
 NPOS = 96
 BLK = 4
 D = NPOS * BLK
+WPR = D // 2
 CH = 16
 NCH = 8
-G = 32
+G = 64
 R = P // G
+CPG = G // CH
+NT = 4
 FLOPS = 2 * NPOS * 128 * 128 * 512
-RAWB = 4
 INV = 1.0 / math.sqrt(128.0)
+
+OFF_XC = 0
+OFF_XS = OFF_XC + 49152
+OFF_A = OFF_XS + 12288
+OFF_S0 = OFF_A + 98304
+OFF_R = OFF_S0 + 49152
+OFF_XG = OFF_R + 2 * 12288
+OFF_ID = OFF_XG + 4 * 2048
+OFF_SC = OFF_ID + 512
+OFF_WC = OFF_A
+OFF_WS = OFF_A + 4 * 6144
+OFF_S1 = OFF_WS + 4 * 1536
+OFF_R2 = OFF_S1 + 49152
+RAW_OFF = [OFF_R, OFF_R + 12288, OFF_R, OFF_R + 12288, OFF_R, OFF_R + 12288, OFF_R2, OFF_R]
+X_ON_VECTOR = 8
 
 
 def tile_nonoverlappinglocallyconnected1d_kernel(tc, x, weight, out):
     nc = tc.nc
     with ExitStack() as ctx:
-        keep = ctx.enter_context(tc.tile_pool(name="keep", bufs=1))
-        rawp = ctx.enter_context(tc.tile_pool(name="rawp", bufs=RAWB))
-        big = ctx.enter_context(tc.tile_pool(name="big", bufs=8))
-        wq = ctx.enter_context(tc.tile_pool(name="wq", bufs=4))
-        psum = ctx.enter_context(tc.psum_pool(name="psum", bufs=8))
+        mem = ctx.enter_context(tc.tile_pool(name="mem", bufs=1))
+        psum = ctx.enter_context(tc.psum_pool(name="psum", bufs=4))
         ctx.enter_context(tc.manual_schedule())
 
-        xcodes = keep.tile([P, NPOS, P], U32, name="xcodes", align_bytes=64)
-        xsc = keep.tile([P, NPOS, P], U8, name="xsc", align_bytes=64)
+        xcodes = mem.tile([P, NPOS, P], U32, name="xcodes", align_bytes=64, offset=OFF_XC)
+        xsc = mem.tile([P, NPOS, P], U8, name="xsc", align_bytes=64, offset=OFF_XS)
+        xraw = mem.tile([P, P * D], BF16, name="xraw", align_bytes=64, offset=OFF_A)
+        ident = mem.tile([P, P], F32, name="ident", align_bytes=64, offset=OFF_ID)
+        scr = mem.tile([P, 8], F32, name="scr", align_bytes=64, offset=OFF_SC)
 
         raws = {}
-        xg = {}
+        xgs = {}
+        tps = {}
         wg = {}
         wcs = {}
         osbs = {}
 
-        def load(k):
-            src = x if k < NCH else weight
-            r0 = CH * (k % NCH)
-            t = rawp.tile([P, CH * D], BF16, tag="raw", name="raw%d" % k)
+        def load_x(c):
             nc.sync.dma_start(
-                out=t[:].rearrange("p (b d) -> p b d", b=CH),
-                in_=src[r0:r0 + CH].rearrange("b i d -> i b d"),
+                out=xraw[:, 32 * D * c:32 * D * (c + 1)],
+                in_=x[:, 32 * c:32 * c + 32, :].rearrange("b i d -> b (i d)"),
+            )
+
+        def load_w(k):
+            t = mem.tile([P, CH * D], BF16, name="raw%d" % k, align_bytes=64, offset=RAW_OFF[k])
+            nc.sync.dma_start(
+                out=t[:].rearrange("p (o d) -> p o d", o=CH),
+                in_=weight[CH * k:CH * k + CH].rearrange("o i d -> i o d"),
             )
             raws[k] = t
 
+        xwords = xraw[:].bitcast(F32).rearrange("p (i w) -> p i w", w=WPR)
+
+        def turn_x(q):
+            tp = psum.tile([P, 4, P], F32, tag="tp", name="tp%d" % q)
+            for m in range(4):
+                nc.tensor.transpose(tp[:, m, :], xwords[:, :, 4 * q + m], ident[:])
+            tps[q] = tp
+
+        def copy_x(q):
+            xg = mem.tile([P, 1024], BF16, name="xg%d" % q, align_bytes=64, offset=OFF_XG + 2048 * (q % 4))
+            xgs[q] = xg
+            o_ap = xg[:].bitcast(F32).rearrange("p (n b u) -> p n b u", n=2, b=P, u=2)
+            i_ap = tps[q][:].rearrange("p (n u) b -> p n b u", n=2, u=2)
+            if q % X_ON_VECTOR == 6:
+                nc.vector.tensor_copy(out=o_ap, in_=i_ap)
+            else:
+                nc.scalar.copy(out=o_ap, in_=i_ap)
+
+        def quant_x(q):
+            nc.vector.quantize_mx(
+                out=xcodes[:, 2 * q:2 * q + 2, :].rearrange("p n b -> p (n b)").bitcast(FP8X4),
+                scales=xsc[:, 2 * q:2 * q + 2, :].rearrange("p n b -> p (n b)"),
+                in_=xgs[q][:],
+            )
+
         def words(k):
-            return raws[k][:].bitcast(F32).rearrange("p (b n u) -> p n b u", b=CH, n=NPOS, u=2)
-
-        def regroup_x(k):
-            h, cc = divmod(k, 4)
-            if cc == 0:
-                xg[h] = [
-                    big.tile([P, 6144], BF16, tag="big", name="xg%d_%d" % (h, q), align_bytes=64)
-                    for q in range(4)
-                ]
-            src = words(k)
-            for q in range(4):
-                dst = xg[h][q][:].bitcast(F32).rearrange("p (n b u) -> p n b u", n=24, b=64, u=2)
-                o_ap = dst[:, :, CH * cc:CH * cc + CH, :]
-                i_ap = src[:, 24 * q:24 * q + 24, :, :]
-                if q == 0:
-                    nc.vector.tensor_copy(out=o_ap, in_=i_ap)
-                else:
-                    nc.scalar.copy(out=o_ap, in_=i_ap)
-
-        def quant_x(h, q):
-            for nl in range(24):
-                n = 24 * q + nl
-                nc.vector.quantize_mx(
-                    out=xcodes[:, n, 64 * h:64 * h + 64].bitcast(FP8X4),
-                    scales=xsc[:, n, 64 * h:64 * h + 64],
-                    in_=xg[h][q][:, 256 * nl:256 * nl + 256],
-                )
+            return raws[k][:].bitcast(F32).rearrange("p (o n u) -> p n o u", o=CH, n=NPOS, u=2)
 
         def regroup_w(k, t, a0, a1, on_scalar):
-            gi, oc = divmod(k - NCH, 2)
+            gi, oc = divmod(k, CPG)
             if (gi, t) not in wg:
-                wg[(gi, t)] = big.tile([P, 6144], BF16, tag="big", name="wg%d_%d" % (gi, t), align_bytes=64)
+                wg[(gi, t)] = mem.tile(
+                    [P, 6144], BF16, name="wg%d_%d" % (gi, t), align_bytes=64,
+                    offset=(OFF_S0 if gi == 0 else OFF_S1) + 12288 * t,
+                )
             dst = wg[(gi, t)][:].bitcast(F32).rearrange("p (w r o u) -> p r w o u", w=12, r=R, o=G, u=2)
-            src = words(k)[:, 48 * t:48 * t + 48, :, :].rearrange("p (r w) o u -> p r w o u", r=R)
+            src = words(k)[:, 24 * t:24 * t + 24, :, :].rearrange("p (r w) o u -> p r w o u", r=R)
             if on_scalar:
                 for r in range(R):
                     nc.scalar.copy(
@@ -98,10 +123,14 @@ def tile_nonoverlappinglocallyconnected1d_kernel(tc, x, weight, out):
                     in_=src[:, :, 4 * a0:4 * a1, :, :],
                 )
 
+        def regroup_all(k, on_scalar):
+            for t in range(NT):
+                regroup_w(k, t, 0, 3, on_scalar)
+
         def quant_w(gi, t, a):
             if a == 0:
-                wc = wq.tile([P, 1536], U32, tag="wc", name="wc%d_%d" % (gi, t), align_bytes=64)
-                ws = wq.tile([P, 1536], U8, tag="ws", name="ws%d_%d" % (gi, t), align_bytes=64)
+                wc = mem.tile([P, 1536], U32, name="wc%d_%d" % (gi, t), align_bytes=64, offset=OFF_WC + 6144 * t)
+                ws = mem.tile([P, 1536], U8, name="ws%d_%d" % (gi, t), align_bytes=64, offset=OFF_WS + 1536 * t)
                 wcs[(gi, t)] = (wc, ws)
             wc, ws = wcs[(gi, t)]
             nc.vector.quantize_mx(
@@ -112,11 +141,11 @@ def tile_nonoverlappinglocallyconnected1d_kernel(tc, x, weight, out):
 
         def passes(gi, t, a):
             if gi not in osbs:
-                osbs[gi] = big.tile([P, G, NPOS], F32, tag="big", name="osb%d" % gi, align_bytes=64)
+                osbs[gi] = mem.tile([P, G, NPOS], F32, name="osb%d" % gi, align_bytes=64, offset=OFF_S0 + 24576 * gi)
             osb = osbs[gi]
             wc, ws = wcs[(gi, t)]
             for r in range(R):
-                n0 = 48 * t + 12 * r + 4 * a
+                n0 = 24 * t + 12 * r + 4 * a
                 ps = psum.tile([P, 4, P], F32, tag="ps", name="ps%d_%d_%d_%d" % (gi, t, a, r))
                 for j in range(4):
                     wl = 4 * a + j
@@ -135,40 +164,50 @@ def tile_nonoverlappinglocallyconnected1d_kernel(tc, x, weight, out):
                     mul=INV,
                 )
 
-        def next_load(k):
-            if k + RAWB < 2 * NCH:
-                load(k + RAWB)
+        for c in range(4):
+            load_x(c)
+        load_w(0)
+        load_w(1)
+        make_identity(nc, ident[:])
+        nc.scalar.copy(out=scr[:], in_=ident[:, 0:8])
+        nc.scalar.mul(out=scr[:], in_=ident[:, 0:8], mul=INV)
 
-        for k in range(RAWB):
-            load(k)
-        for k in range(NCH):
-            regroup_x(k)
-            next_load(k)
-            if k == 3:
-                quant_x(0, 0)
-                quant_x(0, 1)
-            elif k == 4:
-                quant_x(0, 2)
-            elif k == 5:
-                quant_x(0, 3)
-            elif k == 7:
-                for q in range(4):
-                    quant_x(1, q)
-        regroup_w(NCH, 0, 0, 3, True)
-        regroup_w(NCH, 1, 0, 3, True)
-        next_load(NCH)
-        for gi in range(4):
-            k = NCH + 2 * gi + 1
-            regroup_w(k, 0, 0, 1, False)
-            for s in range(6):
-                if s < 5:
-                    regroup_w(k, (s + 1) // 3, (s + 1) % 3, (s + 1) % 3 + 1, False)
-                quant_w(gi, s // 3, s % 3)
-                passes(gi, s // 3, s % 3)
-            next_load(k)
-            if gi < 3:
-                regroup_w(k + 1, 0, 0, 3, False)
-                regroup_w(k + 1, 1, 0, 3, False)
-                next_load(k + 1)
-        for gi in range(4):
+        after = {9: 0, 18: 1, 27: 2, 36: 3}
+        for q in range(48):
+            turn_x(q)
+            copy_x(q)
+            if q >= 1:
+                quant_x(q - 1)
+            if q in after:
+                regroup_all(after[q], False)
+                load_w(after[q] + 2)
+        quant_x(47)
+
+        load_w(6)
+        for a in range(3):
+            quant_w(0, 0, a)
+        for a in range(3):
+            quant_w(0, 1, a)
+        regroup_all(4, False)
+        load_w(7)
+        regroup_all(5, True)
+        for a in range(3):
+            passes(0, 0, a)
+        for a in range(3):
+            quant_w(0, 2, a)
+            passes(0, 1, a)
+        for a in range(3):
+            quant_w(0, 3, a)
+            passes(0, 2, a)
+        regroup_all(6, False)
+        for a in range(3):
+            passes(0, 3, a)
+
+        regroup_w(7, 0, 0, 1, False)
+        for s in range(12):
+            if s < 11:
+                regroup_w(7, (s + 1) // 3, (s + 1) % 3, (s + 1) % 3 + 1, False)
+            quant_w(1, s // 3, s % 3)
+            passes(1, s // 3, s % 3)
+        for gi in range(2):
             nc.sync.dma_start(out=out[:, G * gi:G * gi + G, :], in_=osbs[gi][:])

@@ -74,12 +74,15 @@ def tile_nonoverlappinglocallyconnected1d_kernel(tc, x, weight, out):
             )
             raws[k] = t
 
+        dm = psum.tile([P, 4, P], F32, tag="ps", name="dm")
         xwords = xraw[:].bitcast(F32).rearrange("p (i w) -> p i w", w=WPR)
 
         def turn_x(q):
             tp = psum.tile([P, 4, P], F32, tag="tp", name="tp%d" % q)
             for m in range(4):
                 nc.tensor.transpose(tp[:, m, :], xwords[:, :, 4 * q + m], ident[:])
+            if q % 4 != 3:
+                nc.tensor.matmul(out=dm[:, 0, :], lhsT=ident[:], rhs=ident[:], start=True, stop=True)
             tps[q] = tp
 
         def copy_x(q):

@@ -21,6 +21,9 @@ G = 64
 R = P // G
 CPG = G // CH
 NT = 4
+XCH = 8
+NXC = P // XCH
+XBUF = 8
 FLOPS = 2 * NPOS * 128 * 128 * 512
 INV = 1.0 / math.sqrt(128.0)
 
@@ -49,7 +52,7 @@ def tile_nonoverlappinglocallyconnected1d_kernel(tc, x, weight, out):
 
         xcodes = mem.tile([P, NPOS, P], U32, name="xcodes", align_bytes=64, offset=OFF_XC)
         xsc = mem.tile([P, NPOS, P], U8, name="xsc", align_bytes=64, offset=OFF_XS)
-        xraw = mem.tile([P, P * D], BF16, name="xraw", align_bytes=64, offset=OFF_A)
+        xre = mem.tile([P, P * D], BF16, name="xre", align_bytes=64, offset=OFF_A)
         ident = mem.tile([P, P], F32, name="ident", align_bytes=64, offset=OFF_ID)
         scr = mem.tile([P, 8], F32, name="scr", align_bytes=64, offset=OFF_SC)
 
@@ -60,11 +63,17 @@ def tile_nonoverlappinglocallyconnected1d_kernel(tc, x, weight, out):
         wcs = {}
         osbs = {}
 
+        xrs = {}
+
         def load_x(c):
-            nc.sync.dma_start(
-                out=xraw[:, 32 * D * c:32 * D * (c + 1)],
-                in_=x[:, 32 * c:32 * c + 32, :].rearrange("b i d -> b (i d)"),
-            )
+            t = mem.tile([P, XCH * D], BF16, name="xr%d" % c, align_bytes=64, offset=OFF_S0 + 2 * XCH * D * (c % XBUF))
+            nc.sync.dma_start(out=t[:], in_=x[:, XCH * c:XCH * c + XCH, :].rearrange("b i d -> b (i d)"))
+            xrs[c] = t
+
+        def relayout_x(c):
+            src = xrs[c][:].bitcast(F32).rearrange("p (i w) -> p w i", i=XCH, w=WPR)
+            nc.vector.tensor_copy(out=xwords[:, 0:128, XCH * c:XCH * c + XCH], in_=src[:, 0:128, :])
+            nc.scalar.copy(out=xwords[:, 128:WPR, XCH * c:XCH * c + XCH], in_=src[:, 128:WPR, :])
 
         def load_w(k):
             t = mem.tile([P, CH * D], BF16, name="raw%d" % k, align_bytes=64, offset=RAW_OFF[k])
@@ -75,13 +84,13 @@ def tile_nonoverlappinglocallyconnected1d_kernel(tc, x, weight, out):
             raws[k] = t
 
         dm = psum.tile([P, 4, P], F32, tag="ps", name="dm")
-        xwords = xraw[:].bitcast(F32).rearrange("p (i w) -> p i w", w=WPR)
+        xwords = xre[:].bitcast(F32).rearrange("p (w i) -> p w i", i=P)
 
         def turn_x(q):
             tp = psum.tile([P, 4, P], F32, tag="tp", name="tp%d" % q)
             for m in range(4):
-                nc.tensor.transpose(tp[:, m, :], xwords[:, :, 4 * q + m], ident[:])
-            if q % 4 != 3:
+                nc.tensor.transpose(tp[:, m, :], xwords[:, 4 * q + m, :], ident[:])
+            if q % 2 == 1:
                 nc.tensor.matmul(out=dm[:, 0, :], lhsT=ident[:], rhs=ident[:], start=True, stop=True)
             tps[q] = tp
 
@@ -167,13 +176,21 @@ def tile_nonoverlappinglocallyconnected1d_kernel(tc, x, weight, out):
                     mul=INV,
                 )
 
-        for c in range(4):
+        for c in range(XBUF):
             load_x(c)
-        load_w(0)
-        load_w(1)
         make_identity(nc, ident[:])
         nc.scalar.copy(out=scr[:], in_=ident[:, 0:8])
         nc.scalar.mul(out=scr[:], in_=ident[:, 0:8], mul=INV)
+        for c in range(NXC):
+            relayout_x(c)
+            if c + XBUF < NXC:
+                load_x(c + XBUF)
+            if c + XBUF == NXC - 1:
+                load_w(0)
+                load_w(1)
+            if c == NXC - 3:
+                for e in range(8):
+                    nc.tensor.matmul(out=dm[:, 0, :], lhsT=ident[:], rhs=xrs[c][:].bitcast(F32)[:, 0:P], start=True, stop=True)
 
         after = {9: 0, 18: 1, 27: 2, 36: 3}
         for q in range(48):

@@ -15,12 +15,11 @@ NPOS = 96
 BLK = 4
 D = NPOS * BLK
 WPR = D // 2
-CH = 16
-NCH = 8
+WCH = 8
+NWC = P // WCH
+WBUF = 4
 G = 64
-R = P // G
-CPG = G // CH
-NT = 4
+CPG = G // WCH
 XCH = 8
 NXC = P // XCH
 XBUF = 8
@@ -32,22 +31,19 @@ OFF_XS = OFF_XC + 49152
 OFF_A = OFF_XS + 12288
 OFF_S0 = OFF_A + 98304
 OFF_R = OFF_S0 + 49152
-OFF_XG = OFF_R + 2 * 12288
+OFF_XG = OFF_R + WBUF * 2 * WCH * D
 OFF_ID = OFF_XG + 4 * 2048
 OFF_SC = OFF_ID + 512
 OFF_WC = OFF_A
-OFF_WS = OFF_A + 4 * 6144
-OFF_S1 = OFF_WS + 4 * 1536
-OFF_R2 = OFF_S1 + 49152
-RAW_OFF = [OFF_R, OFF_R + 12288, OFF_R, OFF_R + 12288, OFF_R, OFF_R + 12288, OFF_R2, OFF_R]
-X_ON_VECTOR = 8
+OFF_WS = OFF_A + 2 * 12288
+OFF_S1 = OFF_WS + 2 * 3072
 
 
 def tile_nonoverlappinglocallyconnected1d_kernel(tc, x, weight, out):
     nc = tc.nc
     with ExitStack() as ctx:
         mem = ctx.enter_context(tc.tile_pool(name="mem", bufs=1))
-        psum = ctx.enter_context(tc.psum_pool(name="psum", bufs=4))
+        psum = ctx.enter_context(tc.psum_pool(name="psum", bufs=7))
         ctx.enter_context(tc.manual_schedule())
 
         xcodes = mem.tile([P, NPOS, P], U32, name="xcodes", align_bytes=64, offset=OFF_XC)
@@ -55,7 +51,9 @@ def tile_nonoverlappinglocallyconnected1d_kernel(tc, x, weight, out):
         xre = mem.tile([P, P * D], BF16, name="xre", align_bytes=64, offset=OFF_A)
         ident = mem.tile([P, P], F32, name="ident", align_bytes=64, offset=OFF_ID)
         scr = mem.tile([P, 8], F32, name="scr", align_bytes=64, offset=OFF_SC)
+        dm = psum.tile([P, 4, P], F32, tag="dm", name="dm", bufs=1)
 
+        xrs = {}
         raws = {}
         xgs = {}
         tps = {}
@@ -63,31 +61,29 @@ def tile_nonoverlappinglocallyconnected1d_kernel(tc, x, weight, out):
         wcs = {}
         osbs = {}
 
-        xrs = {}
-
         def load_x(c):
             t = mem.tile([P, XCH * D], BF16, name="xr%d" % c, align_bytes=64, offset=OFF_S0 + 2 * XCH * D * (c % XBUF))
             nc.sync.dma_start(out=t[:], in_=x[:, XCH * c:XCH * c + XCH, :].rearrange("b i d -> b (i d)"))
             xrs[c] = t
 
         def relayout_x(c):
-            src = xrs[c][:].bitcast(F32).rearrange("p (i w) -> p w i", i=XCH, w=WPR)
-            nc.vector.tensor_copy(out=xwords[:, 0:128, XCH * c:XCH * c + XCH], in_=src[:, 0:128, :])
-            nc.scalar.copy(out=xwords[:, 128:WPR, XCH * c:XCH * c + XCH], in_=src[:, 128:WPR, :])
+            src = xrs[c][:].bitcast(F32).rearrange("p (i wb w4) -> p wb i w4", i=XCH, wb=48, w4=4)
+            dst = xre[:].bitcast(F32).rearrange("p (wb w4 i) -> p wb i w4", wb=48, w4=4, i=P)
+            nc.vector.tensor_copy(out=dst[:, 0:32, XCH * c:XCH * c + XCH, :], in_=src[:, 0:32, :, :])
+            nc.scalar.copy(out=dst[:, 32:48, XCH * c:XCH * c + XCH, :], in_=src[:, 32:48, :, :])
 
         def load_w(k):
-            t = mem.tile([P, CH * D], BF16, name="raw%d" % k, align_bytes=64, offset=RAW_OFF[k])
+            t = mem.tile([P, WCH * D], BF16, name="raw%d" % k, align_bytes=64, offset=OFF_R + 2 * WCH * D * (k % WBUF))
             nc.sync.dma_start(
-                out=t[:].rearrange("p (o d) -> p o d", o=CH),
-                in_=weight[CH * k:CH * k + CH].rearrange("o i d -> i o d"),
+                out=t[:].rearrange("p (o d) -> p o d", o=WCH),
+                in_=weight[WCH * k:WCH * k + WCH].rearrange("o i d -> i o d"),
             )
             raws[k] = t
 
-        dm = psum.tile([P, 4, P], F32, tag="ps", name="dm")
         xwords = xre[:].bitcast(F32).rearrange("p (w i) -> p w i", i=P)
 
         def turn_x(q):
-            tp = psum.tile([P, 4, P], F32, tag="tp", name="tp%d" % q)
+            tp = psum.tile([P, 4, P], F32, tag="ps", name="tp%d" % q)
             for m in range(4):
                 nc.tensor.transpose(tp[:, m, :], xwords[:, 4 * q + m, :], ident[:])
             if q % 2 == 1:
@@ -97,12 +93,10 @@ def tile_nonoverlappinglocallyconnected1d_kernel(tc, x, weight, out):
         def copy_x(q):
             xg = mem.tile([P, 1024], BF16, name="xg%d" % q, align_bytes=64, offset=OFF_XG + 2048 * (q % 4))
             xgs[q] = xg
-            o_ap = xg[:].bitcast(F32).rearrange("p (n b u) -> p n b u", n=2, b=P, u=2)
-            i_ap = tps[q][:].rearrange("p (n u) b -> p n b u", n=2, u=2)
-            if q % X_ON_VECTOR == 6:
-                nc.vector.tensor_copy(out=o_ap, in_=i_ap)
-            else:
-                nc.scalar.copy(out=o_ap, in_=i_ap)
+            nc.scalar.copy(
+                out=xg[:].bitcast(F32).rearrange("p (n b u) -> p n b u", n=2, b=P, u=2),
+                in_=tps[q][:].rearrange("p (n u) b -> p n b u", n=2, u=2),
+            )
 
         def quant_x(q):
             nc.vector.quantize_mx(
@@ -111,56 +105,55 @@ def tile_nonoverlappinglocallyconnected1d_kernel(tc, x, weight, out):
                 in_=xgs[q][:],
             )
 
-        def words(k):
-            return raws[k][:].bitcast(F32).rearrange("p (o n u) -> p n o u", o=CH, n=NPOS, u=2)
-
-        def regroup_w(k, t, a0, a1, on_scalar):
+        def regroup_w(k, h, b0, b1, on_scalar):
             gi, oc = divmod(k, CPG)
-            if (gi, t) not in wg:
-                wg[(gi, t)] = mem.tile(
-                    [P, 6144], BF16, name="wg%d_%d" % (gi, t), align_bytes=64,
-                    offset=(OFF_S0 if gi == 0 else OFF_S1) + 12288 * t,
+            if (gi, h) not in wg:
+                wg[(gi, h)] = mem.tile(
+                    [P, 12288], BF16, name="wg%d_%d" % (gi, h), align_bytes=64,
+                    offset=(OFF_S0 if gi == 0 else OFF_S1) + 24576 * h,
                 )
-            dst = wg[(gi, t)][:].bitcast(F32).rearrange("p (w r o u) -> p r w o u", w=12, r=R, o=G, u=2)
-            src = words(k)[:, 24 * t:24 * t + 24, :, :].rearrange("p (r w) o u -> p r w o u", r=R)
+            dst = wg[(gi, h)][:].bitcast(F32).rearrange("p (nb n2 o u) -> p nb o n2 u", nb=24, n2=2, o=G, u=2)
+            src = raws[k][:].bitcast(F32).rearrange("p (o nb n2 u) -> p nb o n2 u", o=WCH, nb=48, n2=2, u=2)
             if on_scalar:
-                for r in range(R):
+                for e in range(2):
                     nc.scalar.copy(
-                        out=dst[:, r, 4 * a0:4 * a1, CH * oc:CH * oc + CH, :],
-                        in_=src[:, r, 4 * a0:4 * a1, :, :],
+                        out=dst[:, b0:b1, WCH * oc:WCH * oc + WCH, e, :],
+                        in_=src[:, 24 * h + b0:24 * h + b1, :, e, :],
                     )
             else:
                 nc.vector.tensor_copy(
-                    out=dst[:, :, 4 * a0:4 * a1, CH * oc:CH * oc + CH, :],
-                    in_=src[:, :, 4 * a0:4 * a1, :, :],
+                    out=dst[:, b0:b1, WCH * oc:WCH * oc + WCH, :, :],
+                    in_=src[:, 24 * h + b0:24 * h + b1, :, :, :],
                 )
 
         def regroup_all(k, on_scalar):
-            for t in range(NT):
-                regroup_w(k, t, 0, 3, on_scalar)
+            regroup_w(k, 0, 0, 24, on_scalar)
+            regroup_w(k, 1, 0, 24, on_scalar)
 
-        def quant_w(gi, t, a):
+        def quant_w(gi, s):
+            h, a = divmod(s, 6)
             if a == 0:
-                wc = mem.tile([P, 1536], U32, name="wc%d_%d" % (gi, t), align_bytes=64, offset=OFF_WC + 6144 * t)
-                ws = mem.tile([P, 1536], U8, name="ws%d_%d" % (gi, t), align_bytes=64, offset=OFF_WS + 1536 * t)
-                wcs[(gi, t)] = (wc, ws)
-            wc, ws = wcs[(gi, t)]
+                wc = mem.tile([P, 3072], U32, name="wc%d_%d" % (gi, h), align_bytes=64, offset=OFF_WC + 12288 * h)
+                ws = mem.tile([P, 3072], U8, name="ws%d_%d" % (gi, h), align_bytes=64, offset=OFF_WS + 3072 * h)
+                wcs[(gi, h)] = (wc, ws)
+            wc, ws = wcs[(gi, h)]
             nc.vector.quantize_mx(
                 out=wc[:, 512 * a:512 * a + 512].bitcast(FP8X4),
                 scales=ws[:, 512 * a:512 * a + 512],
-                in_=wg[(gi, t)][:, 2048 * a:2048 * a + 2048],
+                in_=wg[(gi, h)][:, 2048 * a:2048 * a + 2048],
             )
 
-        def passes(gi, t, a):
+        def passes(gi, s):
             if gi not in osbs:
                 osbs[gi] = mem.tile([P, G, NPOS], F32, name="osb%d" % gi, align_bytes=64, offset=OFF_S0 + 24576 * gi)
             osb = osbs[gi]
-            wc, ws = wcs[(gi, t)]
-            for r in range(R):
-                n0 = 24 * t + 12 * r + 4 * a
-                ps = psum.tile([P, 4, P], F32, tag="ps", name="ps%d_%d_%d_%d" % (gi, t, a, r))
+            h, a = divmod(s, 6)
+            wc, ws = wcs[(gi, h)]
+            for e in range(2):
+                n0 = 8 * s + 4 * e
+                ps = psum.tile([P, 4, P], F32, tag="ps", name="ps%d_%d_%d" % (gi, s, e))
                 for j in range(4):
-                    wl = 4 * a + j
+                    wl = 4 * a + 2 * e + j // 2
                     nc.tensor.matmul_mx(
                         out=ps[:, j, :],
                         lhsT=xcodes[:, n0 + j, :].bitcast(FP8X4),
@@ -171,8 +164,8 @@ def tile_nonoverlappinglocallyconnected1d_kernel(tc, x, weight, out):
                         stop=True,
                     )
                 nc.scalar.mul(
-                    out=osb[:, :, n0:n0 + 4],
-                    in_=ps[:, :, G * r:G * r + G].rearrange("p j c -> p c j"),
+                    out=osb[:, :, n0:n0 + 4].rearrange("p c (jw r) -> p c jw r", r=2),
+                    in_=ps[:].rearrange("p j c -> p (j c)").rearrange("p (jw s y) -> p y jw s", jw=2, s=4, y=G)[:, :, :, 0:4:3],
                     mul=INV,
                 )
 
@@ -186,13 +179,13 @@ def tile_nonoverlappinglocallyconnected1d_kernel(tc, x, weight, out):
             if c + XBUF < NXC:
                 load_x(c + XBUF)
             if c + XBUF == NXC - 1:
-                load_w(0)
-                load_w(1)
+                for k in range(WBUF):
+                    load_w(k)
             if c == NXC - 3:
                 for e in range(8):
                     nc.tensor.matmul(out=dm[:, 0, :], lhsT=ident[:], rhs=xrs[c][:].bitcast(F32)[:, 0:P], start=True, stop=True)
 
-        after = {9: 0, 18: 1, 27: 2, 36: 3}
+        after = {6: 0, 10: 1, 15: 2, 19: 3, 24: 4, 28: 5, 32: 6, 37: 7}
         for q in range(48):
             turn_x(q)
             copy_x(q)
@@ -200,34 +193,36 @@ def tile_nonoverlappinglocallyconnected1d_kernel(tc, x, weight, out):
                 quant_x(q - 1)
             if q in after:
                 regroup_all(after[q], False)
-                load_w(after[q] + 2)
+                load_w(after[q] + WBUF)
         quant_x(47)
 
-        load_w(6)
-        for a in range(3):
-            quant_w(0, 0, a)
-        for a in range(3):
-            quant_w(0, 1, a)
-        regroup_all(4, False)
-        load_w(7)
-        regroup_all(5, True)
-        for a in range(3):
-            passes(0, 0, a)
-        for a in range(3):
-            quant_w(0, 2, a)
-            passes(0, 1, a)
-        for a in range(3):
-            quant_w(0, 3, a)
-            passes(0, 2, a)
-        regroup_all(6, False)
-        for a in range(3):
-            passes(0, 3, a)
+        regroup_all(8, True)
+        load_w(12)
+        regroup_all(9, True)
+        load_w(13)
+        regroup_all(10, False)
+        load_w(14)
+        regroup_all(11, False)
+        load_w(15)
+        for s in range(6):
+            quant_w(0, s)
+        for s in range(6):
+            passes(0, s)
+            quant_w(0, 6 + s)
+            if s == 1:
+                regroup_all(12, False)
+            if s == 4:
+                regroup_all(13, False)
+        for s in range(6, 12):
+            passes(0, s)
+        regroup_all(14, False)
 
-        regroup_w(7, 0, 0, 1, False)
+        regroup_w(15, 0, 0, 4, False)
+        regroup_w(15, 0, 4, 24, False)
         for s in range(12):
-            if s < 11:
-                regroup_w(7, (s + 1) // 3, (s + 1) % 3, (s + 1) % 3 + 1, False)
-            quant_w(1, s // 3, s % 3)
-            passes(1, s // 3, s % 3)
+            quant_w(1, s)
+            if s == 0:
+                regroup_w(15, 1, 0, 24, False)
+            passes(1, s)
         for gi in range(2):
             nc.sync.dma_start(out=out[:, G * gi:G * gi + G, :], in_=osbs[gi][:])

@@ -34,9 +34,9 @@ OFF_R = OFF_S0 + 49152
 OFF_XG = OFF_R + WBUF * 2 * WCH * D
 OFF_ID = OFF_XG + 4 * 2048
 OFF_SC = OFF_ID + 512
-OFF_WC = OFF_A
-OFF_WS = OFF_A + 2 * 12288
-OFF_S1 = OFF_WS + 2 * 3072
+OFF_S1 = OFF_A
+OFF_WC = [OFF_A + 49152, OFF_A + 67584]
+OFF_WS = OFF_A + 61440
 
 
 def tile_nonoverlappinglocallyconnected1d_kernel(tc, x, weight, out):
@@ -133,7 +133,7 @@ def tile_nonoverlappinglocallyconnected1d_kernel(tc, x, weight, out):
         def quant_w(gi, s):
             h, a = divmod(s, 6)
             if a == 0:
-                wc = mem.tile([P, 3072], U32, name="wc%d_%d" % (gi, h), align_bytes=64, offset=OFF_WC + 12288 * h)
+                wc = mem.tile([P, 3072], U32, name="wc%d_%d" % (gi, h), align_bytes=64, offset=OFF_WC[h])
                 ws = mem.tile([P, 3072], U8, name="ws%d_%d" % (gi, h), align_bytes=64, offset=OFF_WS + 3072 * h)
                 wcs[(gi, h)] = (wc, ws)
             wc, ws = wcs[(gi, h)]
@@ -185,7 +185,7 @@ def tile_nonoverlappinglocallyconnected1d_kernel(tc, x, weight, out):
                 for e in range(8):
                     nc.tensor.matmul(out=dm[:, 0, :], lhsT=ident[:], rhs=xrs[c][:].bitcast(F32)[:, 0:P], start=True, stop=True)
 
-        after = {6: 0, 10: 1, 15: 2, 19: 3, 24: 4, 28: 5, 32: 6, 37: 7}
+        after = {6: 0, 10: 1, 15: 2, 19: 3, 24: 4, 28: 5, 32: 6, 36: 7, 39: 8, 42: 9, 45: 10}
         for q in range(48):
             turn_x(q)
             copy_x(q)
@@ -196,13 +196,7 @@ def tile_nonoverlappinglocallyconnected1d_kernel(tc, x, weight, out):
                 load_w(after[q] + WBUF)
         quant_x(47)
 
-        regroup_all(8, True)
-        load_w(12)
-        regroup_all(9, True)
-        load_w(13)
-        regroup_all(10, False)
-        load_w(14)
-        regroup_all(11, False)
+        regroup_all(11, True)
         load_w(15)
         for s in range(6):
             quant_w(0, s)

@@ -51,7 +51,6 @@ def tile_nonoverlappinglocallyconnected1d_kernel(tc, x, weight, out):
         xre = mem.tile([P, P * D], BF16, name="xre", align_bytes=64, offset=OFF_A)
         ident = mem.tile([P, P], F32, name="ident", align_bytes=64, offset=OFF_ID)
         scr = mem.tile([P, 8], F32, name="scr", align_bytes=64, offset=OFF_SC)
-        dm = psum.tile([P, 4, P], F32, tag="dm", name="dm", bufs=1)
 
         xrs = {}
         raws = {}
@@ -86,8 +85,6 @@ def tile_nonoverlappinglocallyconnected1d_kernel(tc, x, weight, out):
             tp = psum.tile([P, 4, P], F32, tag="ps", name="tp%d" % q)
             for m in range(4):
                 nc.tensor.transpose(tp[:, m, :], xwords[:, 4 * q + m, :], ident[:])
-            if q % 2 == 1:
-                nc.tensor.matmul(out=dm[:, 0, :], lhsT=ident[:], rhs=ident[:], start=True, stop=True)
             tps[q] = tp
 
         def copy_x(q):
@@ -181,9 +178,6 @@ def tile_nonoverlappinglocallyconnected1d_kernel(tc, x, weight, out):
             if c + XBUF == NXC - 1:
                 for k in range(WBUF):
                     load_w(k)
-            if c == NXC - 3:
-                for e in range(8):
-                    nc.tensor.matmul(out=dm[:, 0, :], lhsT=ident[:], rhs=xrs[c][:].bitcast(F32)[:, 0:P], start=True, stop=True)
 
         after = {6: 0, 10: 1, 15: 2, 19: 3, 24: 4, 28: 5, 32: 6, 36: 7, 39: 8, 42: 9, 45: 10}
         for q in range(48):

from contextlib import ExitStack
import math

import concourse.mybir as mybir
from concourse.masks import make_identity

F32 = mybir.dt.float32
BF16 = mybir.dt.bfloat16
U32 = mybir.dt.uint32
U8 = mybir.dt.uint8
FP8X4 = mybir.dt.float8_e4m3fn_x4

P = 128
NPOS = 96
BLK = 4
D = NPOS * BLK
WPR = D // 2
WCH = 8
NWC = P // WCH
WBUF = 4
G = 64
CPG = G // WCH
XCH = 8
NXC = P // XCH
XBUF = 8
FLOPS = 2 * NPOS * 128 * 128 * 512
INV = 1.0 / math.sqrt(128.0)

OFF_XC = 0
OFF_XS = OFF_XC + 49152
OFF_A = OFF_XS + 12288
OFF_S0 = OFF_A + 98304
OFF_R = OFF_S0 + 49152
OFF_XG = OFF_R + WBUF * 2 * WCH * D
OFF_ID = OFF_XG + 4 * 2048
OFF_SC = OFF_ID + 512
OFF_S1 = OFF_A
OFF_WC = [OFF_A + 49152, OFF_A + 67584]
OFF_WS = OFF_A + 61440


def tile_nonoverlappinglocallyconnected1d_kernel(tc, x, weight, out):
    nc = tc.nc
    with ExitStack() as ctx:
        mem = ctx.enter_context(tc.tile_pool(name="mem", bufs=1))
        psum = ctx.enter_context(tc.psum_pool(name="psum", bufs=7))
        ctx.enter_context(tc.manual_schedule())

        xcodes = mem.tile([P, NPOS, P], U32, name="xcodes", align_bytes=64, offset=OFF_XC)
        xsc = mem.tile([P, NPOS, P], U8, name="xsc", align_bytes=64, offset=OFF_XS)
        xre = mem.tile([P, P * D], BF16, name="xre", align_bytes=64, offset=OFF_A)
        ident = mem.tile([P, P], F32, name="ident", align_bytes=64, offset=OFF_ID)
        scr = mem.tile([P, 8], F32, name="scr", align_bytes=64, offset=OFF_SC)

        xrs = {}
        raws = {}
        xgs = {}
        tps = {}
        wg = {}
        wcs = {}
        osbs = {}

        def load_x(c):
            t = mem.tile([P, XCH * D], BF16, name="xr%d" % c, align_bytes=64, offset=OFF_S0 + 2 * XCH * D * (c % XBUF))
            nc.sync.dma_start(out=t[:], in_=x[:, XCH * c:XCH * c + XCH, :].rearrange("b i d -> b (i d)"))
            xrs[c] = t

        def relayout_x(c):
            src = xrs[c][:].bitcast(F32).rearrange("p (i wb w4) -> p wb i w4", i=XCH, wb=48, w4=4)
            dst = xre[:].bitcast(F32).rearrange("p (wb w4 i) -> p wb i w4", wb=48, w4=4, i=P)
            nc.vector.tensor_copy(out=dst[:, 0:32, XCH * c:XCH * c + XCH, :], in_=src[:, 0:32, :, :])
            nc.scalar.copy(out=dst[:, 32:48, XCH * c:XCH * c + XCH, :], in_=src[:, 32:48, :, :])

        def load_w(k):
            t = mem.tile([P, WCH * D], BF16, name="raw%d" % k, align_bytes=64, offset=OFF_R + 2 * WCH * D * (k % WBUF))
            nc.sync.dma_start(
                out=t[:].rearrange("p (o d) -> p o d", o=WCH),
                in_=weight[WCH * k:WCH * k + WCH].rearrange("o i d -> i o d"),
            )
            raws[k] = t

        xwords = xre[:].bitcast(F32).rearrange("p (w i) -> p w i", i=P)

        def turn_x(q):
            tp = psum.tile([P, 4, P], F32, tag="ps", name="tp%d" % q)
            for m in range(4):
                nc.tensor.transpose(tp[:, m, :], xwords[:, 4 * q + m, :], ident[:])
            tps[q] = tp

        def copy_x(q):
            xg = mem.tile([P, 1024], BF16, name="xg%d" % q, align_bytes=64, offset=OFF_XG + 2048 * (q % 4))
            xgs[q] = xg
            nc.scalar.copy(
                out=xg[:].bitcast(F32).rearrange("p (n b u) -> p n b u", n=2, b=P, u=2),
                in_=tps[q][:].rearrange("p (n u) b -> p n b u", n=2, u=2),
            )

        def quant_x(q):
            nc.vector.quantize_mx(
                out=xcodes[:, 2 * q:2 * q + 2, :].rearrange("p n b -> p (n b)").bitcast(FP8X4),
                scales=xsc[:, 2 * q:2 * q + 2, :].rearrange("p n b -> p (n b)"),
                in_=xgs[q][:],
            )

        def regroup_w(k, h, b0, b1, on_scalar):
            gi, oc = divmod(k, CPG)
            if (gi, h) not in wg:
                wg[(gi, h)] = mem.tile(
                    [P, 12288], BF16, name="wg%d_%d" % (gi, h), align_bytes=64,
                    offset=(OFF_S0 if gi == 0 else OFF_S1) + 24576 * h,
                )
            dst = wg[(gi, h)][:].bitcast(F32).rearrange("p (nb n2 o u) -> p nb o n2 u", nb=24, n2=2, o=G, u=2)
            src = raws[k][:].bitcast(F32).rearrange("p (o nb n2 u) -> p nb o n2 u", o=WCH, nb=48, n2=2, u=2)
            if on_scalar:
                for e in range(2):
                    nc.scalar.copy(
                        out=dst[:, b0:b1, WCH * oc:WCH * oc + WCH, e, :],
                        in_=src[:, 24 * h + b0:24 * h + b1, :, e, :],
                    )
            else:
                nc.vector.tensor_copy(
                    out=dst[:, b0:b1, WCH * oc:WCH * oc + WCH, :, :],
                    in_=src[:, 24 * h + b0:24 * h + b1, :, :, :],
                )

        def regroup_all(k, on_scalar):
            regroup_w(k, 0, 0, 24, on_scalar)
            regroup_w(k, 1, 0, 24, on_scalar)

        def quant_w(gi, s):
            h, a = divmod(s, 6)
            if a == 0:
                wc = mem.tile([P, 3072], U32, name="wc%d_%d" % (gi, h), align_bytes=64, offset=OFF_WC[h])
                ws = mem.tile([P, 3072], U8, name="ws%d_%d" % (gi, h), align_bytes=64, offset=OFF_WS + 3072 * h)
                wcs[(gi, h)] = (wc, ws)
            wc, ws = wcs[(gi, h)]
            nc.vector.quantize_mx(
                out=wc[:, 512 * a:512 * a + 512].bitcast(FP8X4),
                scales=ws[:, 512 * a:512 * a + 512],
                in_=wg[(gi, h)][:, 2048 * a:2048 * a + 2048],
            )

        def passes(gi, s):
            if gi not in osbs:
                osbs[gi] = mem.tile([P, G, NPOS], F32, name="osb%d" % gi, align_bytes=64, offset=OFF_S0 + 24576 * gi)
            osb = osbs[gi]
            h, a = divmod(s, 6)
            wc, ws = wcs[(gi, h)]
            for e in range(2):
                n0 = 8 * s + 4 * e
                ps = psum.tile([P, 4, P], F32, tag="ps", name="ps%d_%d_%d" % (gi, s, e))
                for j in range(4):
                    wl = 4 * a + 2 * e + j // 2
                    nc.tensor.matmul_mx(
                        out=ps[:, j, :],
                        lhsT=xcodes[:, n0 + j, :].bitcast(FP8X4),
                        lhsT_scale=xsc[:, n0 + j, :],
                        rhs=wc[:, P * wl:P * wl + P].bitcast(FP8X4),
                        rhs_scale=ws[:, P * wl:P * wl + P],
                        start=True,
                        stop=True,
                    )
                nc.scalar.mul(
                    out=osb[:, :, n0:n0 + 4].rearrange("p c (jw r) -> p c jw r", r=2),
                    in_=ps[:].rearrange("p j c -> p (j c)").rearrange("p (jw s y) -> p y jw s", jw=2, s=4, y=G)[:, :, :, 0:4:3],
                    mul=INV,
                )

        for c in range(XBUF):
            load_x(c)
        make_identity(nc, ident[:])
        nc.scalar.copy(out=scr[:], in_=ident[:, 0:8])
        nc.scalar.mul(out=scr[:], in_=ident[:, 0:8], mul=INV)
        for c in range(NXC):
            relayout_x(c)
            if c + XBUF < NXC:
                load_x(c + XBUF)
            if c + XBUF == NXC - 1:
                for k in range(WBUF):
                    load_w(k)

        after = {6: 0, 10: 1, 15: 2, 19: 3, 24: 4, 28: 5, 32: 6, 36: 7, 39: 8, 42: 9, 45: 10}
        for q in range(48):
            turn_x(q)
            copy_x(q)
            if q >= 1:
                quant_x(q - 1)
            if q in after:
                regroup_all(after[q], False)
                load_w(after[q] + WBUF)
        quant_x(47)

        regroup_all(11, True)
        load_w(15)
        for s in range(6):
            quant_w(0, s)
        for s in range(6):
            passes(0, s)
            quant_w(0, 6 + s)
            if s == 1:
                regroup_all(12, False)
            if s == 4:
                regroup_all(13, False)
        for s in range(6, 12):
            passes(0, s)
        regroup_all(14, False)

        regroup_w(15, 0, 0, 4, False)
        regroup_w(15, 0, 4, 24, False)
        for s in range(12):
            quant_w(1, s)
            if s == 0:
                regroup_w(15, 1, 0, 24, False)
            passes(1, s)
        for gi in range(2):
            nc.sync.dma_start(out=out[:, G * gi:G * gi + G, :], in_=osbs[gi][:])
